import numpy as np
import ml_dtypes


def mxq(x, axis, fmt="e4m3"):
    dtype, down = {"e4m3": (ml_dtypes.float8_e4m3fn, 7), "e5m2": (ml_dtypes.float8_e5m2, 14)}[fmt]
    v = np.moveaxis(np.asarray(x, np.float32).astype(ml_dtypes.bfloat16).astype(np.float64), axis, -1)
    blocks = v.reshape(v.shape[:-1] + (-1, 32))
    amax = np.abs(blocks).max(-1, keepdims=True)
    byte = np.maximum(np.where(amax > 0, np.frexp(amax)[1] - 1 + 127, 0) - down, 1)
    scale = np.exp2(byte - 127.0)
    codes = (blocks / scale).astype(np.float32).astype(dtype).astype(np.float64)
    return np.moveaxis((codes * scale).reshape(v.shape), -1, axis)


WIDE = False


def mx_kscale(k):
    if not WIDE:
        return np.ones(k)
    levels = np.array([10, -10, 5, -5, 0])
    a = np.random.permutation(np.resize(levels, k // 512 * 4)).reshape(k // 512, 4)
    idx = np.arange(k)
    return np.exp2(a[idx // 512, idx % 128 // 32])


BF16 = ml_dtypes.bfloat16


def bf(x):
    return np.asarray(x, np.float32).astype(BF16)


def f64(x):
    return np.asarray(x).astype(np.float64)


B, N, DIM, HEADS, DIM_HEAD = 2, 512, 1024, 16, 64
INNER = HEADS * DIM_HEAD


def setup_inputs():
    s = mx_kscale(DIM)
    return {"x": bf(np.random.standard_normal((B, N, DIM)) * s),
            "W": bf(np.random.standard_normal((3 * INNER, DIM)) / np.sqrt(DIM) / s[None, :])}


def reference(x, W):
    b, n, _ = x.shape
    qkv = mxq(f64(x), 2, "e4m3") @ mxq(f64(W), 1, "e4m3").T
    q, k, v = np.split(qkv, 3, axis=-1)

    def to_heads(t):
        return t.reshape(b, n, HEADS, DIM_HEAD).transpose(0, 2, 1, 3)

    return to_heads(q), to_heads(k), to_heads(v)

@@ -1,0 +1,168 @@
+from contextlib import ExitStack
+
+import concourse.bass as bass
+import concourse.mybir as mybir
+import concourse.tile as tile
+from concourse.masks import make_identity
+
+F32 = mybir.dt.float32
+BF16 = mybir.dt.bfloat16
+U32 = mybir.dt.uint32
+U8 = mybir.dt.uint8
+FP8X4 = mybir.dt.float8_e4m3fn_x4
+
+P = 128
+K = 1024
+TOK = 1024
+E = 3072
+FLOPS = 2 * TOK * K * E
+
+SETS = 8
+WBLK = 6
+PIN = True
+
+
+def tile_get_qkv_kernel(tc, x, W, out_0, out_1, out_2):
+    nc = tc.nc
+    outs = [out_0, out_1, out_2]
+    with ExitStack() as ctx:
+        keep = ctx.enter_context(tc.tile_pool(name="keep", bufs=1))
+        rot = ctx.enter_context(tc.tile_pool(name="rot", bufs=3))
+        psum = ctx.enter_context(tc.psum_pool(name="psum", bufs=1))
+        if PIN:
+            ctx.enter_context(tc.manual_schedule())
+
+        counter = [0]
+
+        def new_bank():
+            i = counter[0] % 8
+            counter[0] += 1
+            return psum.tile([P, 512], F32, name="bank%d" % i, tag="bank%d" % i)
+
+        x_sb = keep.tile([P, SETS * K], BF16, name="x_sb")
+        w_sb = [keep.tile([P, 4 * K], BF16, name="w_sb%d" % wb) for wb in range(WBLK)]
+
+        def load_x(half):
+            for b in range(2):
+                src = x[b].rearrange("(q s) k -> q (s k)", s=SETS)
+                cols = slice(half * 4 * K, (half + 1) * 4 * K)
+                nc.sync.dma_start(out=x_sb[b:P:2, cols], in_=src[:, cols])
+
+        def load_w(wb):
+            src = W[wb * 512:(wb + 1) * 512, :].rearrange("(p t) k -> p (t k)", t=4)
+            nc.sync.dma_start(out=w_sb[wb][:], in_=src)
+
+        load_x(0)
+        load_w(0)
+        load_x(1)
+        for wb in range(1, WBLK):
+            load_w(wb)
+
+        ident = keep.tile([P, P], F32, name="ident")
+        make_identity(nc, ident[:])
+
+        xg = keep.tile([P, SETS * K], BF16, name="xg", align_bytes=64)
+        x_codes = keep.tile([P, SETS * 256], U32, name="x_codes", align_bytes=64)
+        x_scales = keep.tile([P, SETS * 256], U8, name="x_scales", align_bytes=64)
+        x32 = x_sb[:].bitcast(F32)
+        xg32 = xg[:].bitcast(F32)
+
+        def copy_out(eng, dst, bank):
+            src = bank[:].rearrange("p (g u c) -> p g c u", g=2, u=2)
+            if eng == 0:
+                nc.vector.tensor_copy(out=dst, in_=src)
+            else:
+                nc.scalar.copy(out=dst, in_=src)
+
+        def transpose_x(half):
+            for s in range(half * 4, half * 4 + 4):
+                bank = new_bank()
+                for j in range(4):
+                    nc.tensor.transpose(
+                        bank[:, j * P:(j + 1) * P],
+                        x32[:, s * 512 + j * P: s * 512 + (j + 1) * P],
+                        ident[:],
+                    )
+                dst = xg32[:, s * 512:(s + 1) * 512].rearrange(
+                    "p (g c u) -> p g c u", g=2, u=2)
+                copy_out(s % 2, dst, bank)
+            nc.vector.quantize_mx(
+                out=x_codes[:, half * 1024:(half + 1) * 1024].bitcast(FP8X4),
+                scales=x_scales[:, half * 1024:(half + 1) * 1024],
+                in_=xg[:, half * 4096:(half + 1) * 4096],
+            )
+
+        w_codes = {}
+        w_scales = {}
+
+        def transpose_w(wb, engines):
+            w32 = w_sb[wb][:].bitcast(F32)
+            wg = rot.tile([P, 4096], BF16, name="wg", tag="wg", align_bytes=64)
+            wg32 = wg[:].bitcast(F32).rearrange(
+                "p (g t c u) -> p g t c u", g=2, t=4, u=2)
+            for t in range(4):
+                bank = new_bank()
+                for j in range(4):
+                    nc.tensor.transpose(
+                        bank[:, j * P:(j + 1) * P],
+                        w32[:, t * 512 + j * P: t * 512 + (j + 1) * P],
+                        ident[:],
+                    )
+                copy_out(engines[t], wg32[:, :, t, :, :], bank)
+            codes = rot.tile([P, 1024], U32, name="wc", tag="wc", align_bytes=64)
+            scales = rot.tile([P, 1024], U8, name="ws", tag="ws", align_bytes=64)
+            for g in range(2):
+                nc.vector.quantize_mx(
+                    out=codes[:, g * 512:(g + 1) * 512].bitcast(FP8X4),
+                    scales=scales[:, g * 512:(g + 1) * 512],
+                    in_=wg[:, g * 2048:(g + 1) * 2048],
+                )
+            w_codes[wb] = codes
+            w_scales[wb] = scales
+
+        o_sb = {}
+
+        def multiply(wb, sets):
+            if wb not in o_sb:
+                o_sb[wb] = keep.tile([P, 4096], F32, name="o_sb%d" % wb)
+            o_view = o_sb[wb][:].rearrange(
+                "p (h s q t) -> p h s q t", h=8, s=SETS, q=16, t=4)
+            for s in sets:
+                acc = new_bank()
+                for g in range(2):
+                    nc.tensor.matmul_mx(
+                        out=acc[:],
+                        lhsT=x_codes[:, s * 256 + g * P: s * 256 + (g + 1) * P].bitcast(FP8X4),
+                        lhsT_scale=x_scales[:, s * 256 + g * P: s * 256 + (g + 1) * P],
+                        rhs=w_codes[wb][:, g * 512:(g + 1) * 512].bitcast(FP8X4),
+                        rhs_scale=w_scales[wb][:, g * 512:(g + 1) * 512],
+                        start=(g == 0),
+                        stop=(g == 1),
+                    )
+                nc.scalar.copy(
+                    out=o_view[:, :, s, :, :],
+                    in_=acc[:].rearrange("p (t h q) -> p h q t", t=4, h=8, q=16),
+                )
+
+        def store(wb):
+            dst_all = outs[wb // 2]
+            h0 = (wb % 2) * 8
+            for b in range(2):
+                dst = dst_all[b, h0:h0 + 8].rearrange("h (q s) d -> q h (s d)", s=SETS)
+                nc.sync.dma_start(
+                    out=dst,
+                    in_=o_sb[wb][b:P:2, :].rearrange("p (h r) -> p h r", h=8),
+                )
+
+        transpose_x(0)
+        transpose_w(0, [0, 1, 0, 1])
+        transpose_x(1)
+        multiply(0, range(0, 4))
+        transpose_w(1, [0, 0, 0, 0])
+        multiply(0, range(4, 8))
+        store(0)
+        for wb in range(1, WBLK):
+            if wb + 1 < WBLK:
+                transpose_w(wb + 1, [0, 0, 0, 0])
+            multiply(wb, range(SETS))
+            store(wb)

@@ -1,8 +1,6 @@
 from contextlib import ExitStack
 
-import concourse.bass as bass
 import concourse.mybir as mybir
-import concourse.tile as tile
 from concourse.masks import make_identity
 
 F32 = mybir.dt.float32
@@ -19,7 +17,9 @@ FLOPS = 2 * TOK * K * E
 
 SETS = 8
 WBLK = 6
-PIN = True
+NATURAL = (5,)
+V = 0
+S = 1
 
 
 def tile_get_qkv_kernel(tc, x, W, out_0, out_1, out_2):
@@ -29,8 +29,7 @@ def tile_get_qkv_kernel(tc, x, W, out_0, out_1, out_2):
         keep = ctx.enter_context(tc.tile_pool(name="keep", bufs=1))
         rot = ctx.enter_context(tc.tile_pool(name="rot", bufs=3))
         psum = ctx.enter_context(tc.psum_pool(name="psum", bufs=1))
-        if PIN:
-            ctx.enter_context(tc.manual_schedule())
+        ctx.enter_context(tc.manual_schedule())
 
         counter = [0]
 
@@ -39,76 +38,74 @@ def tile_get_qkv_kernel(tc, x, W, out_0, out_1, out_2):
             counter[0] += 1
             return psum.tile([P, 512], F32, name="bank%d" % i, tag="bank%d" % i)
 
-        x_sb = keep.tile([P, SETS * K], BF16, name="x_sb")
-        w_sb = [keep.tile([P, 4 * K], BF16, name="w_sb%d" % wb) for wb in range(WBLK)]
+        x_sb = [keep.tile([P, 2 * K], BF16, name="x_sb%d" % i) for i in range(4)]
+        w_sb = {}
 
-        def load_x(half):
+        def load_x(part):
             for b in range(2):
                 src = x[b].rearrange("(q s) k -> q (s k)", s=SETS)
-                cols = slice(half * 4 * K, (half + 1) * 4 * K)
-                nc.sync.dma_start(out=x_sb[b:P:2, cols], in_=src[:, cols])
+                nc.sync.dma_start(out=x_sb[part][b:P:2, :],
+                                  in_=src[:, part * 2 * K:(part + 1) * 2 * K])
 
-        def load_w(wb):
-            src = W[wb * 512:(wb + 1) * 512, :].rearrange("(p t) k -> p (t k)", t=4)
-            nc.sync.dma_start(out=w_sb[wb][:], in_=src)
+        def load_w(wb, pieces):
+            rows = W[wb * 512:(wb + 1) * 512, :]
+            n = 4 // pieces
+            for i in range(pieces):
+                w_t = keep.tile([P, n * K], BF16, name="w_sb%d_%d" % (wb, i))
+                if wb in NATURAL:
+                    src = rows.rearrange("(t p) k -> p t k", p=P)[:, i * n:(i + 1) * n, :]
+                    nc.sync.dma_start(out=w_t[:].rearrange("p (t k) -> p t k", t=n), in_=src)
+                else:
+                    src = rows.rearrange("(p t) k -> p (t k)", t=4)[:, i * n * K:(i + 1) * n * K]
+                    nc.sync.dma_start(out=w_t[:], in_=src)
+                for j in range(n):
+                    w_sb[(wb, i * n + j)] = w_t[:].bitcast(F32)[:, j * 512:(j + 1) * 512]
 
         load_x(0)
-        load_w(0)
         load_x(1)
+        load_w(0, 2)
+        load_x(2)
+        load_x(3)
         for wb in range(1, WBLK):
-            load_w(wb)
+            load_w(wb, 1)
 
         ident = keep.tile([P, P], F32, name="ident")
         make_identity(nc, ident[:])
 
-        xg = keep.tile([P, SETS * K], BF16, name="xg", align_bytes=64)
-        x_codes = keep.tile([P, SETS * 256], U32, name="x_codes", align_bytes=64)
-        x_scales = keep.tile([P, SETS * 256], U8, name="x_scales", align_bytes=64)
-        x32 = x_sb[:].bitcast(F32)
-        xg32 = xg[:].bitcast(F32)
+        xg = [keep.tile([P, 2 * K], BF16, name="xg%d" % i, align_bytes=64) for i in range(4)]
+        x_codes = [keep.tile([P, 512], U32, name="x_codes%d" % i, align_bytes=64) for i in range(4)]
+        x_scales = [keep.tile([P, 512], U8, name="x_scales%d" % i, align_bytes=64) for i in range(4)]
 
-        def copy_out(eng, dst, bank):
-            src = bank[:].rearrange("p (g u c) -> p g c u", g=2, u=2)
-            if eng == 0:
+        def copy(eng, dst, src):
+            if eng == V:
                 nc.vector.tensor_copy(out=dst, in_=src)
             else:
                 nc.scalar.copy(out=dst, in_=src)
 
-        def transpose_x(half):
-            for s in range(half * 4, half * 4 + 4):
-                bank = new_bank()
-                for j in range(4):
-                    nc.tensor.transpose(
-                        bank[:, j * P:(j + 1) * P],
-                        x32[:, s * 512 + j * P: s * 512 + (j + 1) * P],
-                        ident[:],
-                    )
-                dst = xg32[:, s * 512:(s + 1) * 512].rearrange(
-                    "p (g c u) -> p g c u", g=2, u=2)
-                copy_out(s % 2, dst, bank)
-            nc.vector.quantize_mx(
-                out=x_codes[:, half * 1024:(half + 1) * 1024].bitcast(FP8X4),
-                scales=x_scales[:, half * 1024:(half + 1) * 1024],
-                in_=xg[:, half * 4096:(half + 1) * 4096],
-            )
+        def transpose4(words):
+            bank = new_bank()
+            for j in range(4):
+                nc.tensor.transpose(bank[:, j * P:(j + 1) * P], words[:, j * P:(j + 1) * P], ident[:])
+            return bank[:].rearrange("p (g u c) -> p g c u", g=2, u=2)
+
+        def transpose_x(s, eng):
+            src = transpose4(x_sb[s // 2][:].bitcast(F32)[:, (s % 2) * 512:(s % 2 + 1) * 512])
+            dst = xg[s // 2][:].bitcast(F32)[:, (s % 2) * 512:(s % 2 + 1) * 512]
+            copy(eng, dst.rearrange("p (g c u) -> p g c u", g=2, u=2), src)
+
+        def quantise_x(part):
+            nc.vector.quantize_mx(out=x_codes[part][:].bitcast(FP8X4), scales=x_scales[part][:],
+                                  in_=xg[part][:])
 
         w_codes = {}
         w_scales = {}
 
         def transpose_w(wb, engines):
-            w32 = w_sb[wb][:].bitcast(F32)
             wg = rot.tile([P, 4096], BF16, name="wg", tag="wg", align_bytes=64)
-            wg32 = wg[:].bitcast(F32).rearrange(
-                "p (g t c u) -> p g t c u", g=2, t=4, u=2)
+            wg32 = wg[:].bitcast(F32).rearrange("p (g t c u) -> p g t c u", g=2, t=4, u=2)
             for t in range(4):
-                bank = new_bank()
-                for j in range(4):
-                    nc.tensor.transpose(
-                        bank[:, j * P:(j + 1) * P],
-                        w32[:, t * 512 + j * P: t * 512 + (j + 1) * P],
-                        ident[:],
-                    )
-                copy_out(engines[t], wg32[:, :, t, :, :], bank)
+                src = transpose4(w_sb[(wb, t)])
+                copy(engines[t], wg32[:, :, t, :, :], src)
             codes = rot.tile([P, 1024], U32, name="wc", tag="wc", align_bytes=64)
             scales = rot.tile([P, 1024], U8, name="ws", tag="ws", align_bytes=64)
             for g in range(2):
@@ -120,49 +117,88 @@ def tile_get_qkv_kernel(tc, x, W, out_0, out_1, out_2):
             w_codes[wb] = codes
             w_scales[wb] = scales
 
+        def mx_pass(acc, s, g, wb, c0, n):
+            off = (s % 2) * 256 + g * P
+            nc.tensor.matmul_mx(
+                out=acc,
+                lhsT=x_codes[s // 2][:, off:off + P].bitcast(FP8X4),
+                lhsT_scale=x_scales[s // 2][:, off:off + P],
+                rhs=w_codes[wb][:, g * 512 + c0:g * 512 + c0 + n].bitcast(FP8X4),
+                rhs_scale=w_scales[wb][:, g * 512 + c0:g * 512 + c0 + n],
+                start=(g == 0),
+                stop=(g == 1),
+            )
+
         o_sb = {}
 
-        def multiply(wb, sets):
+        def copy_product(wb, s, acc, eng):
+            if wb in NATURAL:
+                dst = o_sb[wb][:].rearrange("p (h s d) -> p h s d", h=8, s=SETS)[:, :, s, :]
+                src = acc[:].rearrange("p (h d) -> p h d", h=8)
+            else:
+                dst = o_sb[wb][:].rearrange(
+                    "p (h s q t) -> p h s q t", h=8, s=SETS, q=16, t=4)[:, :, s, :, :]
+                src = acc[:].rearrange("p (t h q) -> p h q t", t=4, h=8, q=16)
+            copy(eng, dst, src)
+
+        def multiply(wb, sets, g_major=False):
             if wb not in o_sb:
                 o_sb[wb] = keep.tile([P, 4096], F32, name="o_sb%d" % wb)
-            o_view = o_sb[wb][:].rearrange(
-                "p (h s q t) -> p h s q t", h=8, s=SETS, q=16, t=4)
-            for s in sets:
-                acc = new_bank()
+            if g_major:
+                accs = [new_bank() for s in sets]
                 for g in range(2):
-                    nc.tensor.matmul_mx(
-                        out=acc[:],
-                        lhsT=x_codes[:, s * 256 + g * P: s * 256 + (g + 1) * P].bitcast(FP8X4),
-                        lhsT_scale=x_scales[:, s * 256 + g * P: s * 256 + (g + 1) * P],
-                        rhs=w_codes[wb][:, g * 512:(g + 1) * 512].bitcast(FP8X4),
-                        rhs_scale=w_scales[wb][:, g * 512:(g + 1) * 512],
-                        start=(g == 0),
-                        stop=(g == 1),
-                    )
-                nc.scalar.copy(
-                    out=o_view[:, :, s, :, :],
-                    in_=acc[:].rearrange("p (t h q) -> p h q t", t=4, h=8, q=16),
-                )
+                    for i, s in enumerate(sets):
+                        mx_pass(accs[i][:], s, g, wb, 0, 512)
+                for i, s in enumerate(sets):
+                    copy_product(wb, s, accs[i], S)
+            else:
+                for s in sets:
+                    acc = new_bank()
+                    for g in range(2):
+                        mx_pass(acc[:], s, g, wb, 0, 512)
+                    copy_product(wb, s, acc, S)
 
         def store(wb):
-            dst_all = outs[wb // 2]
             h0 = (wb % 2) * 8
             for b in range(2):
-                dst = dst_all[b, h0:h0 + 8].rearrange("h (q s) d -> q h (s d)", s=SETS)
-                nc.sync.dma_start(
-                    out=dst,
-                    in_=o_sb[wb][b:P:2, :].rearrange("p (h r) -> p h r", h=8),
-                )
+                dst = outs[wb // 2][b, h0:h0 + 8].rearrange("h (q s) d -> q h (s d)", s=SETS)
+                nc.sync.dma_start(out=dst, in_=o_sb[wb][b:P:2, :].rearrange("p (h r) -> p h r", h=8))
 
-        transpose_x(0)
-        transpose_w(0, [0, 1, 0, 1])
-        transpose_x(1)
-        multiply(0, range(0, 4))
-        transpose_w(1, [0, 0, 0, 0])
-        multiply(0, range(4, 8))
+        def multiply_tail(wb):
+            for t in range(4):
+                o_t = keep.tile([P, 2 * SETS * 64], F32, name="o_tail%d" % t)
+                o_view = o_t[:].rearrange("p (h s d) -> p h s d", h=2, s=SETS)
+                for half in range(2):
+                    acc = new_bank()
+                    for i in range(4):
+                        for g in range(2):
+                            mx_pass(acc[:, i * P:(i + 1) * P], half * 4 + i, g, wb, t * P, P)
+                    copy(S if half == 0 else V, o_view[:, :, half * 4:(half + 1) * 4, :],
+                         acc[:].rearrange("p (s h d) -> p h s d", s=4, h=2))
+                h0 = (wb % 2) * 8 + 2 * t
+                for b in range(2):
+                    dst = outs[wb // 2][b, h0:h0 + 2].rearrange("h (q s) d -> q h (s d)", s=SETS)
+                    nc.sync.dma_start(out=dst, in_=o_t[b:P:2, :].rearrange("p (h r) -> p h r", h=2))
+
+        transpose_x(0, V)
+        transpose_x(1, S)
+        transpose_x(2, V)
+        transpose_x(3, S)
+        quantise_x(0)
+        quantise_x(1)
+        transpose_w(0, [V, S, V, S])
+        multiply(0, [0, 1, 2, 3], g_major=True)
+        transpose_x(4, V)
+        transpose_x(5, S)
+        transpose_x(6, V)
+        transpose_x(7, S)
+        quantise_x(2)
+        quantise_x(3)
+        transpose_w(1, [V, V, V, V])
+        multiply(0, [4, 5, 6, 7])
         store(0)
-        for wb in range(1, WBLK):
-            if wb + 1 < WBLK:
-                transpose_w(wb + 1, [0, 0, 0, 0])
+        for wb in range(1, WBLK - 1):
+            transpose_w(wb + 1, [V, V, V, V])
             multiply(wb, range(SETS))
             store(wb)
+        multiply_tail(WBLK - 1)

@@ -17,7 +17,6 @@ FLOPS = 2 * TOK * K * E
 
 SETS = 8
 WBLK = 6
-NATURAL = (5,)
 V = 0
 S = 1
 
@@ -48,16 +47,11 @@ def tile_get_qkv_kernel(tc, x, W, out_0, out_1, out_2):
                                   in_=src[:, part * 2 * K:(part + 1) * 2 * K])
 
         def load_w(wb, pieces):
-            rows = W[wb * 512:(wb + 1) * 512, :]
+            rows = W[wb * 512:(wb + 1) * 512, :].rearrange("(p t) k -> p (t k)", t=4)
             n = 4 // pieces
             for i in range(pieces):
                 w_t = keep.tile([P, n * K], BF16, name="w_sb%d_%d" % (wb, i))
-                if wb in NATURAL:
-                    src = rows.rearrange("(t p) k -> p t k", p=P)[:, i * n:(i + 1) * n, :]
-                    nc.sync.dma_start(out=w_t[:].rearrange("p (t k) -> p t k", t=n), in_=src)
-                else:
-                    src = rows.rearrange("(p t) k -> p (t k)", t=4)[:, i * n * K:(i + 1) * n * K]
-                    nc.sync.dma_start(out=w_t[:], in_=src)
+                nc.sync.dma_start(out=w_t[:], in_=rows[:, i * n * K:(i + 1) * n * K])
                 for j in range(n):
                     w_sb[(wb, i * n + j)] = w_t[:].bitcast(F32)[:, j * 512:(j + 1) * 512]
 
@@ -86,12 +80,13 @@ def tile_get_qkv_kernel(tc, x, W, out_0, out_1, out_2):
             bank = new_bank()
             for j in range(4):
                 nc.tensor.transpose(bank[:, j * P:(j + 1) * P], words[:, j * P:(j + 1) * P], ident[:])
-            return bank[:].rearrange("p (g u c) -> p g c u", g=2, u=2)
+            return bank
 
         def transpose_x(s, eng):
-            src = transpose4(x_sb[s // 2][:].bitcast(F32)[:, (s % 2) * 512:(s % 2 + 1) * 512])
+            bank = transpose4(x_sb[s // 2][:].bitcast(F32)[:, (s % 2) * 512:(s % 2 + 1) * 512])
             dst = xg[s // 2][:].bitcast(F32)[:, (s % 2) * 512:(s % 2 + 1) * 512]
-            copy(eng, dst.rearrange("p (g c u) -> p g c u", g=2, u=2), src)
+            copy(eng, dst.rearrange("p (g c u) -> p g c u", g=2, u=2),
+                 bank[:].rearrange("p (g u c) -> p g c u", g=2, u=2))
 
         def quantise_x(part):
             nc.vector.quantize_mx(out=x_codes[part][:].bitcast(FP8X4), scales=x_scales[part][:],
@@ -100,85 +95,59 @@ def tile_get_qkv_kernel(tc, x, W, out_0, out_1, out_2):
         w_codes = {}
         w_scales = {}
 
-        def transpose_w(wb, engines):
+        def transpose_w(wb, engines, q_calls):
             wg = rot.tile([P, 4096], BF16, name="wg", tag="wg", align_bytes=64)
-            wg32 = wg[:].bitcast(F32).rearrange("p (g t c u) -> p g t c u", g=2, t=4, u=2)
+            wg32 = wg[:].bitcast(F32).rearrange(
+                "p (g a t c u) -> p g a t c u", g=2, a=2, t=4, c=64, u=2)
             for t in range(4):
-                src = transpose4(w_sb[(wb, t)])
-                copy(engines[t], wg32[:, :, t, :, :], src)
+                bank = transpose4(w_sb[(wb, t)])
+                copy(engines[t], wg32[:, :, :, t, :, :],
+                     bank[:].rearrange("p (g u a c) -> p g a c u", g=2, u=2, a=2, c=64))
             codes = rot.tile([P, 1024], U32, name="wc", tag="wc", align_bytes=64)
             scales = rot.tile([P, 1024], U8, name="ws", tag="ws", align_bytes=64)
-            for g in range(2):
+            for c0, n in q_calls:
                 nc.vector.quantize_mx(
-                    out=codes[:, g * 512:(g + 1) * 512].bitcast(FP8X4),
-                    scales=scales[:, g * 512:(g + 1) * 512],
-                    in_=wg[:, g * 2048:(g + 1) * 2048],
+                    out=codes[:, c0:c0 + n].bitcast(FP8X4),
+                    scales=scales[:, c0:c0 + n],
+                    in_=wg[:, 4 * c0:4 * (c0 + n)],
                 )
             w_codes[wb] = codes
             w_scales[wb] = scales
 
-        def mx_pass(acc, s, g, wb, c0, n):
+        def mx_pass(acc, s, g, wb, a):
             off = (s % 2) * 256 + g * P
+            c0 = g * 512 + a * 256
             nc.tensor.matmul_mx(
                 out=acc,
                 lhsT=x_codes[s // 2][:, off:off + P].bitcast(FP8X4),
                 lhsT_scale=x_scales[s // 2][:, off:off + P],
-                rhs=w_codes[wb][:, g * 512 + c0:g * 512 + c0 + n].bitcast(FP8X4),
-                rhs_scale=w_scales[wb][:, g * 512 + c0:g * 512 + c0 + n],
+                rhs=w_codes[wb][:, c0:c0 + 256].bitcast(FP8X4),
+                rhs_scale=w_scales[wb][:, c0:c0 + 256],
                 start=(g == 0),
                 stop=(g == 1),
             )
 
         o_sb = {}
 
-        def copy_product(wb, s, acc, eng):
-            if wb in NATURAL:
-                dst = o_sb[wb][:].rearrange("p (h s d) -> p h s d", h=8, s=SETS)[:, :, s, :]
-                src = acc[:].rearrange("p (h d) -> p h d", h=8)
-            else:
-                dst = o_sb[wb][:].rearrange(
-                    "p (h s q t) -> p h s q t", h=8, s=SETS, q=16, t=4)[:, :, s, :, :]
-                src = acc[:].rearrange("p (t h q) -> p h q t", t=4, h=8, q=16)
-            copy(eng, dst, src)
-
-        def multiply(wb, sets, g_major=False):
-            if wb not in o_sb:
-                o_sb[wb] = keep.tile([P, 4096], F32, name="o_sb%d" % wb)
-            if g_major:
-                accs = [new_bank() for s in sets]
-                for g in range(2):
-                    for i, s in enumerate(sets):
-                        mx_pass(accs[i][:], s, g, wb, 0, 512)
-                for i, s in enumerate(sets):
-                    copy_product(wb, s, accs[i], S)
-            else:
-                for s in sets:
-                    acc = new_bank()
+        def multiply(wb, a, pairs, engines):
+            if (wb, a) not in o_sb:
+                o_sb[(wb, a)] = keep.tile([P, 2048], F32, name="o_sb%d_%d" % (wb, a))
+            o_view = o_sb[(wb, a)][:].rearrange(
+                "p (h s q t) -> p s h q t", h=4, s=SETS, q=16, t=4)
+            for n, pair in enumerate(pairs):
+                acc = new_bank()
+                for i in range(2):
                     for g in range(2):
-                        mx_pass(acc[:], s, g, wb, 0, 512)
-                    copy_product(wb, s, acc, S)
+                        mx_pass(acc[:, i * 256:(i + 1) * 256], 2 * pair + i, g, wb, a)
+                copy(engines[n], o_view[:, 2 * pair:2 * pair + 2, :, :, :],
+                     acc[:].rearrange("p (i t h q) -> p i h q t", i=2, t=4, h=4, q=16))
 
-        def store(wb):
-            h0 = (wb % 2) * 8
+        def store(wb, a, s0, s1):
+            h0 = (wb % 2) * 8 + a * 4
             for b in range(2):
-                dst = outs[wb // 2][b, h0:h0 + 8].rearrange("h (q s) d -> q h (s d)", s=SETS)
-                nc.sync.dma_start(out=dst, in_=o_sb[wb][b:P:2, :].rearrange("p (h r) -> p h r", h=8))
-
-        def multiply_tail(wb):
-            for t in range(4):
-                o_t = keep.tile([P, 2 * SETS * 64], F32, name="o_tail%d" % t)
-                o_view = o_t[:].rearrange("p (h s d) -> p h s d", h=2, s=SETS)
-                for half in range(2):
-                    acc = new_bank()
-                    for i in range(4):
-                        for g in range(2):
-                            mx_pass(acc[:, i * P:(i + 1) * P], half * 4 + i, g, wb, t * P, P)
-                    copy(S if half == 0 else V, o_view[:, :, half * 4:(half + 1) * 4, :],
-                         acc[:].rearrange("p (s h d) -> p h s d", s=4, h=2))
-                h0 = (wb % 2) * 8 + 2 * t
-                for b in range(2):
-                    dst = outs[wb // 2][b, h0:h0 + 2].rearrange("h (q s) d -> q h (s d)", s=SETS)
-                    nc.sync.dma_start(out=dst, in_=o_t[b:P:2, :].rearrange("p (h r) -> p h r", h=2))
+                dst = outs[wb // 2][b, h0:h0 + 4].rearrange("h (q s) d -> q h s d", s=SETS)
+                src = o_sb[(wb, a)][b:P:2, :].rearrange("p (h s d) -> p h s d", h=4, s=SETS)
+                nc.sync.dma_start(out=dst[:, :, s0:s1, :], in_=src[:, :, s0:s1, :])
 
         transpose_x(0, V)
         transpose_x(1, S)
@@ -186,19 +155,30 @@ def tile_get_qkv_kernel(tc, x, W, out_0, out_1, out_2):
         transpose_x(3, S)
         quantise_x(0)
         quantise_x(1)
-        transpose_w(0, [V, S, V, S])
-        multiply(0, [0, 1, 2, 3], g_major=True)
+        transpose_w(0, [V, S, V, S], [(0, 256), (512, 256), (256, 256), (768, 256)])
+        multiply(0, 0, [0, 1], [S, V])
+        multiply(0, 1, [0, 1], [S, V])
         transpose_x(4, V)
         transpose_x(5, S)
         transpose_x(6, V)
         transpose_x(7, S)
         quantise_x(2)
         quantise_x(3)
-        transpose_w(1, [V, V, V, V])
-        multiply(0, [4, 5, 6, 7])
-        store(0)
-        for wb in range(1, WBLK - 1):
-            transpose_w(wb + 1, [V, V, V, V])
-            multiply(wb, range(SETS))
-            store(wb)
-        multiply_tail(WBLK - 1)
+        transpose_w(1, [V, V, V, V], [(0, 512), (512, 512)])
+        multiply(0, 0, [2, 3], [S, S])
+        store(0, 0, 0, SETS)
+        multiply(0, 1, [2, 3], [S, S])
+        store(0, 1, 0, SETS)
+        for wb in range(1, WBLK):
+            if wb + 1 < WBLK:
+                transpose_w(wb + 1, [V, V, V, V], [(0, 512), (512, 512)])
+            multiply(wb, 0, [0, 1, 2, 3], [S, S, S, V])
+            store(wb, 0, 0, SETS)
+            if wb + 1 < WBLK:
+                multiply(wb, 1, [0, 1, 2, 3], [S, S, S, V])
+                store(wb, 1, 0, SETS)
+            else:
+                multiply(wb, 1, [0, 1], [S, V])
+                store(wb, 1, 0, 4)
+                multiply(wb, 1, [2, 3], [S, V])
+                store(wb, 1, 4, SETS)

@@ -56,8 +56,8 @@ def tile_get_qkv_kernel(tc, x, W, out_0, out_1, out_2):
                     w_sb[(wb, i * n + j)] = w_t[:].bitcast(F32)[:, j * 512:(j + 1) * 512]
 
         load_x(0)
-        load_x(1)
         load_w(0, 2)
+        load_x(1)
         load_x(2)
         load_x(3)
         for wb in range(1, WBLK):
@@ -94,6 +94,7 @@ def tile_get_qkv_kernel(tc, x, W, out_0, out_1, out_2):
 
         w_codes = {}
         w_scales = {}
+        w_grouped = {}
 
         def transpose_w(wb, engines, q_calls):
             wg = rot.tile([P, 4096], BF16, name="wg", tag="wg", align_bytes=64)
@@ -103,16 +104,18 @@ def tile_get_qkv_kernel(tc, x, W, out_0, out_1, out_2):
                 bank = transpose4(w_sb[(wb, t)])
                 copy(engines[t], wg32[:, :, :, t, :, :],
                      bank[:].rearrange("p (g u a c) -> p g a c u", g=2, u=2, a=2, c=64))
-            codes = rot.tile([P, 1024], U32, name="wc", tag="wc", align_bytes=64)
-            scales = rot.tile([P, 1024], U8, name="ws", tag="ws", align_bytes=64)
+            w_codes[wb] = rot.tile([P, 1024], U32, name="wc", tag="wc", align_bytes=64)
+            w_scales[wb] = rot.tile([P, 1024], U8, name="ws", tag="ws", align_bytes=64)
+            w_grouped[wb] = wg
+            quantise_w(wb, q_calls)
+
+        def quantise_w(wb, q_calls):
             for c0, n in q_calls:
                 nc.vector.quantize_mx(
-                    out=codes[:, c0:c0 + n].bitcast(FP8X4),
-                    scales=scales[:, c0:c0 + n],
-                    in_=wg[:, 4 * c0:4 * (c0 + n)],
+                    out=w_codes[wb][:, c0:c0 + n].bitcast(FP8X4),
+                    scales=w_scales[wb][:, c0:c0 + n],
+                    in_=w_grouped[wb][:, 4 * c0:4 * (c0 + n)],
                 )
-            w_codes[wb] = codes
-            w_scales[wb] = scales
 
         def mx_pass(acc, s, g, wb, a):
             off = (s % 2) * 256 + g * P
@@ -149,29 +152,34 @@ def tile_get_qkv_kernel(tc, x, W, out_0, out_1, out_2):
                 src = o_sb[(wb, a)][b:P:2, :].rearrange("p (h s d) -> p h s d", h=4, s=SETS)
                 nc.sync.dma_start(out=dst[:, :, s0:s1, :], in_=src[:, :, s0:s1, :])
 
+        QUARTERS = [(0, 256), (512, 256), (256, 256), (768, 256)]
+        HALVES = [(0, 512), (512, 512)]
         transpose_x(0, V)
         transpose_x(1, S)
+        quantise_x(0)
+        transpose_w(0, [V, S, V, S], QUARTERS[0:2])
         transpose_x(2, V)
         transpose_x(3, S)
-        quantise_x(0)
+        quantise_w(0, QUARTERS[2:4])
         quantise_x(1)
-        transpose_w(0, [V, S, V, S], [(0, 256), (512, 256), (256, 256), (768, 256)])
-        multiply(0, 0, [0, 1], [S, V])
-        multiply(0, 1, [0, 1], [S, V])
+        multiply(0, 0, [0], [S])
+        multiply(0, 1, [0], [S])
+        multiply(0, 0, [1], [S])
+        multiply(0, 1, [1], [V])
         transpose_x(4, V)
         transpose_x(5, S)
         transpose_x(6, V)
         transpose_x(7, S)
         quantise_x(2)
         quantise_x(3)
-        transpose_w(1, [V, V, V, V], [(0, 512), (512, 512)])
+        transpose_w(1, [V, V, S, S], QUARTERS)
         multiply(0, 0, [2, 3], [S, S])
         store(0, 0, 0, SETS)
         multiply(0, 1, [2, 3], [S, S])
         store(0, 1, 0, SETS)
         for wb in range(1, WBLK):
             if wb + 1 < WBLK:
-                transpose_w(wb + 1, [V, V, V, V], [(0, 512), (512, 512)])
+                transpose_w(wb + 1, [V, V, V, V], HALVES)
             multiply(wb, 0, [0, 1, 2, 3], [S, S, S, V])
             store(wb, 0, 0, SETS)
             if wb + 1 < WBLK:
@@ -180,5 +188,7 @@ def tile_get_qkv_kernel(tc, x, W, out_0, out_1, out_2):
             else:
                 multiply(wb, 1, [0, 1], [S, V])
                 store(wb, 1, 0, 4)
-                multiply(wb, 1, [2, 3], [S, V])
-                store(wb, 1, 4, SETS)
+                multiply(wb, 1, [2], [S])
+                store(wb, 1, 4, 6)
+                multiply(wb, 1, [3], [V])
+                store(wb, 1, 6, SETS)

@@ -76,14 +76,22 @@ def tile_get_qkv_kernel(tc, x, W, out_0, out_1, out_2):
             else:
                 nc.scalar.copy(out=dst, in_=src)
 
-        def transpose4(words):
+        zeros = keep.tile([P, 512], BF16, name="zeros")
+        nc.vector.memset(zeros[:], 0.0)
+
+        def warm(bank, n):
+            for i in range(n):
+                nc.tensor.matmul(out=bank[:], lhsT=zeros[:, 0:P], rhs=zeros[:], start=True, stop=True)
+
+        def transpose4(words, n_warm=0):
             bank = new_bank()
+            warm(bank, n_warm)
             for j in range(4):
                 nc.tensor.transpose(bank[:, j * P:(j + 1) * P], words[:, j * P:(j + 1) * P], ident[:])
             return bank
 
-        def transpose_x(s, eng):
-            bank = transpose4(x_sb[s // 2][:].bitcast(F32)[:, (s % 2) * 512:(s % 2 + 1) * 512])
+        def transpose_x(s, eng, n_warm=0):
+            bank = transpose4(x_sb[s // 2][:].bitcast(F32)[:, (s % 2) * 512:(s % 2 + 1) * 512], n_warm)
             dst = xg[s // 2][:].bitcast(F32)[:, (s % 2) * 512:(s % 2 + 1) * 512]
             copy(eng, dst.rearrange("p (g c u) -> p g c u", g=2, u=2),
                  bank[:].rearrange("p (g u c) -> p g c u", g=2, u=2))
@@ -96,12 +104,12 @@ def tile_get_qkv_kernel(tc, x, W, out_0, out_1, out_2):
         w_scales = {}
         w_grouped = {}
 
-        def transpose_w(wb, engines, q_calls):
+        def transpose_w(wb, engines, q_calls, warms=(0, 0, 0, 0)):
             wg = rot.tile([P, 4096], BF16, name="wg", tag="wg", align_bytes=64)
             wg32 = wg[:].bitcast(F32).rearrange(
                 "p (g a t c u) -> p g a t c u", g=2, a=2, t=4, c=64, u=2)
             for t in range(4):
-                bank = transpose4(w_sb[(wb, t)])
+                bank = transpose4(w_sb[(wb, t)], warms[t])
                 copy(engines[t], wg32[:, :, :, t, :, :],
                      bank[:].rearrange("p (g u a c) -> p g a c u", g=2, u=2, a=2, c=64))
             w_codes[wb] = rot.tile([P, 1024], U32, name="wc", tag="wc", align_bytes=64)
@@ -132,13 +140,14 @@ def tile_get_qkv_kernel(tc, x, W, out_0, out_1, out_2):
 
         o_sb = {}
 
-        def multiply(wb, a, pairs, engines):
+        def multiply(wb, a, pairs, engines, n_warm=0):
             if (wb, a) not in o_sb:
                 o_sb[(wb, a)] = keep.tile([P, 2048], F32, name="o_sb%d_%d" % (wb, a))
             o_view = o_sb[(wb, a)][:].rearrange(
                 "p (h s q t) -> p s h q t", h=4, s=SETS, q=16, t=4)
             for n, pair in enumerate(pairs):
                 acc = new_bank()
+                warm(acc, n_warm)
                 for i in range(2):
                     for g in range(2):
                         mx_pass(acc[:, i * 256:(i + 1) * 256], 2 * pair + i, g, wb, a)
@@ -154,15 +163,15 @@ def tile_get_qkv_kernel(tc, x, W, out_0, out_1, out_2):
 
         QUARTERS = [(0, 256), (512, 256), (256, 256), (768, 256)]
         HALVES = [(0, 512), (512, 512)]
-        transpose_x(0, V)
+        transpose_x(0, V, 7)
         transpose_x(1, S)
         quantise_x(0)
-        transpose_w(0, [V, S, V, S], QUARTERS[0:2])
-        transpose_x(2, V)
+        transpose_w(0, [V, S, V, S], QUARTERS[0:2], (2, 0, 2, 0))
+        transpose_x(2, V, 2)
         transpose_x(3, S)
         quantise_w(0, QUARTERS[2:4])
         quantise_x(1)
-        multiply(0, 0, [0], [S])
+        multiply(0, 0, [0], [S], 2)
         multiply(0, 1, [0], [S])
         multiply(0, 0, [1], [S])
         multiply(0, 1, [1], [V])

@@ -76,22 +76,14 @@ def tile_get_qkv_kernel(tc, x, W, out_0, out_1, out_2):
             else:
                 nc.scalar.copy(out=dst, in_=src)
 
-        zeros = keep.tile([P, 512], BF16, name="zeros")
-        nc.vector.memset(zeros[:], 0.0)
-
-        def warm(bank, n):
-            for i in range(n):
-                nc.tensor.matmul(out=bank[:], lhsT=zeros[:, 0:P], rhs=zeros[:], start=True, stop=True)
-
-        def transpose4(words, n_warm=0):
+        def transpose4(words):
             bank = new_bank()
-            warm(bank, n_warm)
             for j in range(4):
                 nc.tensor.transpose(bank[:, j * P:(j + 1) * P], words[:, j * P:(j + 1) * P], ident[:])
             return bank
 
-        def transpose_x(s, eng, n_warm=0):
-            bank = transpose4(x_sb[s // 2][:].bitcast(F32)[:, (s % 2) * 512:(s % 2 + 1) * 512], n_warm)
+        def transpose_x(s, eng):
+            bank = transpose4(x_sb[s // 2][:].bitcast(F32)[:, (s % 2) * 512:(s % 2 + 1) * 512])
             dst = xg[s // 2][:].bitcast(F32)[:, (s % 2) * 512:(s % 2 + 1) * 512]
             copy(eng, dst.rearrange("p (g c u) -> p g c u", g=2, u=2),
                  bank[:].rearrange("p (g u c) -> p g c u", g=2, u=2))
@@ -104,12 +96,12 @@ def tile_get_qkv_kernel(tc, x, W, out_0, out_1, out_2):
         w_scales = {}
         w_grouped = {}
 
-        def transpose_w(wb, engines, q_calls, warms=(0, 0, 0, 0)):
+        def transpose_w(wb, engines, q_calls):
             wg = rot.tile([P, 4096], BF16, name="wg", tag="wg", align_bytes=64)
             wg32 = wg[:].bitcast(F32).rearrange(
                 "p (g a t c u) -> p g a t c u", g=2, a=2, t=4, c=64, u=2)
             for t in range(4):
-                bank = transpose4(w_sb[(wb, t)], warms[t])
+                bank = transpose4(w_sb[(wb, t)])
                 copy(engines[t], wg32[:, :, :, t, :, :],
                      bank[:].rearrange("p (g u a c) -> p g a c u", g=2, u=2, a=2, c=64))
             w_codes[wb] = rot.tile([P, 1024], U32, name="wc", tag="wc", align_bytes=64)
@@ -140,14 +132,13 @@ def tile_get_qkv_kernel(tc, x, W, out_0, out_1, out_2):
 
         o_sb = {}
 
-        def multiply(wb, a, pairs, engines, n_warm=0):
+        def multiply(wb, a, pairs, engines):
             if (wb, a) not in o_sb:
                 o_sb[(wb, a)] = keep.tile([P, 2048], F32, name="o_sb%d_%d" % (wb, a))
             o_view = o_sb[(wb, a)][:].rearrange(
                 "p (h s q t) -> p s h q t", h=4, s=SETS, q=16, t=4)
             for n, pair in enumerate(pairs):
                 acc = new_bank()
-                warm(acc, n_warm)
                 for i in range(2):
                     for g in range(2):
                         mx_pass(acc[:, i * 256:(i + 1) * 256], 2 * pair + i, g, wb, a)
@@ -163,22 +154,28 @@ def tile_get_qkv_kernel(tc, x, W, out_0, out_1, out_2):
 
         QUARTERS = [(0, 256), (512, 256), (256, 256), (768, 256)]
         HALVES = [(0, 512), (512, 512)]
-        transpose_x(0, V, 7)
+
+        def block(wb, engines):
+            for a in range(2):
+                multiply(wb, a, [0, 1, 2, 3], engines)
+                store(wb, a, 0, SETS)
+
+        transpose_x(0, V)
         transpose_x(1, S)
         quantise_x(0)
-        transpose_w(0, [V, S, V, S], QUARTERS[0:2], (2, 0, 2, 0))
-        transpose_x(2, V, 2)
+        transpose_w(0, [V, S, V, S], QUARTERS[0:2])
+        transpose_x(2, V)
         transpose_x(3, S)
         quantise_w(0, QUARTERS[2:4])
         quantise_x(1)
-        multiply(0, 0, [0], [S], 2)
-        multiply(0, 1, [0], [S])
-        multiply(0, 0, [1], [S])
-        multiply(0, 1, [1], [V])
-        transpose_x(4, V)
+        transpose_x(4, S)
         transpose_x(5, S)
+        multiply(0, 0, [0], [S])
+        multiply(0, 1, [0], [S])
         transpose_x(6, V)
-        transpose_x(7, S)
+        transpose_x(7, V)
+        multiply(0, 0, [1], [S])
+        multiply(0, 1, [1], [S])
         quantise_x(2)
         quantise_x(3)
         transpose_w(1, [V, V, S, S], QUARTERS)
@@ -186,18 +183,12 @@ def tile_get_qkv_kernel(tc, x, W, out_0, out_1, out_2):
         store(0, 0, 0, SETS)
         multiply(0, 1, [2, 3], [S, S])
         store(0, 1, 0, SETS)
-        for wb in range(1, WBLK):
-            if wb + 1 < WBLK:
-                transpose_w(wb + 1, [V, V, V, V], HALVES)
-            multiply(wb, 0, [0, 1, 2, 3], [S, S, S, V])
-            store(wb, 0, 0, SETS)
-            if wb + 1 < WBLK:
-                multiply(wb, 1, [0, 1, 2, 3], [S, S, S, V])
-                store(wb, 1, 0, SETS)
-            else:
-                multiply(wb, 1, [0, 1], [S, V])
-                store(wb, 1, 0, 4)
-                multiply(wb, 1, [2], [S])
-                store(wb, 1, 4, 6)
-                multiply(wb, 1, [3], [V])
-                store(wb, 1, 6, SETS)
+        transpose_w(2, [V, V, V, V], HALVES)
+        transpose_w(3, [V, V, V, V], HALVES)
+        block(1, [S, S, S, S])
+        block(2, [S, S, S, V])
+        transpose_w(4, [V, V, V, V], HALVES)
+        transpose_w(5, [V, V, V, V], HALVES)
+        block(3, [S, S, S, S])
+        block(4, [S, S, S, V])
+        block(5, [S, V, S, V])

@@ -17,6 +17,7 @@ FLOPS = 2 * TOK * K * E
 
 SETS = 8
 WBLK = 6
+PAD = 48
 V = 0
 S = 1
 
@@ -67,8 +68,8 @@ def tile_get_qkv_kernel(tc, x, W, out_0, out_1, out_2):
         make_identity(nc, ident[:])
 
         xg = [keep.tile([P, 2 * K], BF16, name="xg%d" % i, align_bytes=64) for i in range(4)]
-        x_codes = [keep.tile([P, 512], U32, name="x_codes%d" % i, align_bytes=64) for i in range(4)]
-        x_scales = [keep.tile([P, 512], U8, name="x_scales%d" % i, align_bytes=64) for i in range(4)]
+        x_codes = [keep.tile([P, PAD + 512], U32, name="x_codes%d" % i, align_bytes=256) for i in range(4)]
+        x_scales = [keep.tile([P, 1024], U8, name="x_scales%d" % i, align_bytes=256) for i in range(4)]
 
         def copy(eng, dst, src):
             if eng == V:
@@ -89,8 +90,11 @@ def tile_get_qkv_kernel(tc, x, W, out_0, out_1, out_2):
                  bank[:].rearrange("p (g u c) -> p g c u", g=2, u=2))
 
         def quantise_x(part):
-            nc.vector.quantize_mx(out=x_codes[part][:].bitcast(FP8X4), scales=x_scales[part][:],
-                                  in_=xg[part][:])
+            for j in range(4):
+                nc.vector.quantize_mx(
+                    out=x_codes[part][:, PAD + j * P:PAD + (j + 1) * P].bitcast(FP8X4),
+                    scales=x_scales[part][:, j * 256:j * 256 + P],
+                    in_=xg[part][:, j * 512:(j + 1) * 512])
 
         w_codes = {}
         w_scales = {}
@@ -104,8 +108,8 @@ def tile_get_qkv_kernel(tc, x, W, out_0, out_1, out_2):
                 bank = transpose4(w_sb[(wb, t)])
                 copy(engines[t], wg32[:, :, :, t, :, :],
                      bank[:].rearrange("p (g u a c) -> p g a c u", g=2, u=2, a=2, c=64))
-            w_codes[wb] = rot.tile([P, 1024], U32, name="wc", tag="wc", align_bytes=64)
-            w_scales[wb] = rot.tile([P, 1024], U8, name="ws", tag="ws", align_bytes=64)
+            w_codes[wb] = rot.tile([P, 1024], U32, name="wc", tag="wc", align_bytes=256)
+            w_scales[wb] = rot.tile([P, 1024], U8, name="ws", tag="ws", align_bytes=256)
             w_grouped[wb] = wg
             quantise_w(wb, q_calls)
 
@@ -118,12 +122,12 @@ def tile_get_qkv_kernel(tc, x, W, out_0, out_1, out_2):
                 )
 
         def mx_pass(acc, s, g, wb, a):
-            off = (s % 2) * 256 + g * P
+            j = (s % 2) * 2 + g
             c0 = g * 512 + a * 256
             nc.tensor.matmul_mx(
                 out=acc,
-                lhsT=x_codes[s // 2][:, off:off + P].bitcast(FP8X4),
-                lhsT_scale=x_scales[s // 2][:, off:off + P],
+                lhsT=x_codes[s // 2][:, PAD + j * P:PAD + (j + 1) * P].bitcast(FP8X4),
+                lhsT_scale=x_scales[s // 2][:, j * 256:j * 256 + P],
                 rhs=w_codes[wb][:, c0:c0 + 256].bitcast(FP8X4),
                 rhs_scale=w_scales[wb][:, c0:c0 + 256],
                 start=(g == 0),

@@ -17,7 +17,6 @@ FLOPS = 2 * TOK * K * E
 
 SETS = 8
 WBLK = 6
-PAD = 48
 V = 0
 S = 1
 
@@ -68,8 +67,8 @@ def tile_get_qkv_kernel(tc, x, W, out_0, out_1, out_2):
         make_identity(nc, ident[:])
 
         xg = [keep.tile([P, 2 * K], BF16, name="xg%d" % i, align_bytes=64) for i in range(4)]
-        x_codes = [keep.tile([P, PAD + 512], U32, name="x_codes%d" % i, align_bytes=256) for i in range(4)]
-        x_scales = [keep.tile([P, 1024], U8, name="x_scales%d" % i, align_bytes=256) for i in range(4)]
+        x_codes = [keep.tile([P, 512], U32, name="x_codes%d" % i, align_bytes=64) for i in range(4)]
+        x_scales = [keep.tile([P, 512], U8, name="x_scales%d" % i, align_bytes=64) for i in range(4)]
 
         def copy(eng, dst, src):
             if eng == V:
@@ -90,11 +89,8 @@ def tile_get_qkv_kernel(tc, x, W, out_0, out_1, out_2):
                  bank[:].rearrange("p (g u c) -> p g c u", g=2, u=2))
 
         def quantise_x(part):
-            for j in range(4):
-                nc.vector.quantize_mx(
-                    out=x_codes[part][:, PAD + j * P:PAD + (j + 1) * P].bitcast(FP8X4),
-                    scales=x_scales[part][:, j * 256:j * 256 + P],
-                    in_=xg[part][:, j * 512:(j + 1) * 512])
+            nc.vector.quantize_mx(out=x_codes[part][:].bitcast(FP8X4), scales=x_scales[part][:],
+                                  in_=xg[part][:])
 
         w_codes = {}
         w_scales = {}
@@ -108,8 +104,8 @@ def tile_get_qkv_kernel(tc, x, W, out_0, out_1, out_2):
                 bank = transpose4(w_sb[(wb, t)])
                 copy(engines[t], wg32[:, :, :, t, :, :],
                      bank[:].rearrange("p (g u a c) -> p g a c u", g=2, u=2, a=2, c=64))
-            w_codes[wb] = rot.tile([P, 1024], U32, name="wc", tag="wc", align_bytes=256)
-            w_scales[wb] = rot.tile([P, 1024], U8, name="ws", tag="ws", align_bytes=256)
+            w_codes[wb] = rot.tile([P, 1024], U32, name="wc", tag="wc", align_bytes=64)
+            w_scales[wb] = rot.tile([P, 1024], U8, name="ws", tag="ws", align_bytes=64)
             w_grouped[wb] = wg
             quantise_w(wb, q_calls)
 
@@ -122,12 +118,12 @@ def tile_get_qkv_kernel(tc, x, W, out_0, out_1, out_2):
                 )
 
         def mx_pass(acc, s, g, wb, a):
-            j = (s % 2) * 2 + g
+            off = (s % 2) * 256 + g * P
             c0 = g * 512 + a * 256
             nc.tensor.matmul_mx(
                 out=acc,
-                lhsT=x_codes[s // 2][:, PAD + j * P:PAD + (j + 1) * P].bitcast(FP8X4),
-                lhsT_scale=x_scales[s // 2][:, j * 256:j * 256 + P],
+                lhsT=x_codes[s // 2][:, off:off + P].bitcast(FP8X4),
+                lhsT_scale=x_scales[s // 2][:, off:off + P],
                 rhs=w_codes[wb][:, c0:c0 + 256].bitcast(FP8X4),
                 rhs_scale=w_scales[wb][:, c0:c0 + 256],
                 start=(g == 0),
@@ -176,23 +172,23 @@ def tile_get_qkv_kernel(tc, x, W, out_0, out_1, out_2):
         transpose_x(5, S)
         multiply(0, 0, [0], [S])
         multiply(0, 1, [0], [S])
-        transpose_x(6, V)
-        transpose_x(7, V)
         multiply(0, 0, [1], [S])
         multiply(0, 1, [1], [S])
         quantise_x(2)
+        transpose_x(6, V)
+        transpose_x(7, V)
         quantise_x(3)
         transpose_w(1, [V, V, S, S], QUARTERS)
+        transpose_w(2, [V, V, V, V], HALVES)
         multiply(0, 0, [2, 3], [S, S])
         store(0, 0, 0, SETS)
         multiply(0, 1, [2, 3], [S, S])
         store(0, 1, 0, SETS)
-        transpose_w(2, [V, V, V, V], HALVES)
+        block(1, [S, S, S, V])
         transpose_w(3, [V, V, V, V], HALVES)
-        block(1, [S, S, S, S])
-        block(2, [S, S, S, V])
         transpose_w(4, [V, V, V, V], HALVES)
+        block(2, [S, S, S, S])
+        block(3, [S, S, S, V])
         transpose_w(5, [V, V, V, V], HALVES)
-        block(3, [S, S, S, S])
         block(4, [S, S, S, V])
         block(5, [S, V, S, V])

from contextlib import ExitStack

import concourse.mybir as mybir
from concourse.masks import make_identity

F32 = mybir.dt.float32
BF16 = mybir.dt.bfloat16
U32 = mybir.dt.uint32
U8 = mybir.dt.uint8
FP8X4 = mybir.dt.float8_e4m3fn_x4

P = 128
K = 1024
TOK = 1024
E = 3072
FLOPS = 2 * TOK * K * E

SETS = 8
WBLK = 6
V = 0
S = 1


def tile_get_qkv_kernel(tc, x, W, out_0, out_1, out_2):
    nc = tc.nc
    outs = [out_0, out_1, out_2]
    with ExitStack() as ctx:
        keep = ctx.enter_context(tc.tile_pool(name="keep", bufs=1))
        rot = ctx.enter_context(tc.tile_pool(name="rot", bufs=3))
        psum = ctx.enter_context(tc.psum_pool(name="psum", bufs=1))
        ctx.enter_context(tc.manual_schedule())

        counter = [0]

        def new_bank():
            i = counter[0] % 8
            counter[0] += 1
            return psum.tile([P, 512], F32, name="bank%d" % i, tag="bank%d" % i)

        x_sb = [keep.tile([P, 2 * K], BF16, name="x_sb%d" % i) for i in range(4)]
        w_sb = {}

        def load_x(part):
            for b in range(2):
                src = x[b].rearrange("(q s) k -> q (s k)", s=SETS)
                nc.sync.dma_start(out=x_sb[part][b:P:2, :],
                                  in_=src[:, part * 2 * K:(part + 1) * 2 * K])

        def load_w(wb, pieces):
            rows = W[wb * 512:(wb + 1) * 512, :].rearrange("(p t) k -> p (t k)", t=4)
            n = 4 // pieces
            for i in range(pieces):
                w_t = keep.tile([P, n * K], BF16, name="w_sb%d_%d" % (wb, i))
                nc.sync.dma_start(out=w_t[:], in_=rows[:, i * n * K:(i + 1) * n * K])
                for j in range(n):
                    w_sb[(wb, i * n + j)] = w_t[:].bitcast(F32)[:, j * 512:(j + 1) * 512]

        load_x(0)
        load_w(0, 2)
        load_x(1)
        load_x(2)
        load_x(3)
        for wb in range(1, WBLK):
            load_w(wb, 1)

        ident = keep.tile([P, P], F32, name="ident")
        make_identity(nc, ident[:])

        xg = [keep.tile([P, 2 * K], BF16, name="xg%d" % i, align_bytes=64) for i in range(4)]
        x_codes = [keep.tile([P, 512], U32, name="x_codes%d" % i, align_bytes=64) for i in range(4)]
        x_scales = [keep.tile([P, 512], U8, name="x_scales%d" % i, align_bytes=64) for i in range(4)]

        def copy(eng, dst, src):
            if eng == V:
                nc.vector.tensor_copy(out=dst, in_=src)
            else:
                nc.scalar.copy(out=dst, in_=src)

        def transpose4(words):
            bank = new_bank()
            for j in range(4):
                nc.tensor.transpose(bank[:, j * P:(j + 1) * P], words[:, j * P:(j + 1) * P], ident[:])
            return bank

        def transpose_x(s, eng):
            bank = transpose4(x_sb[s // 2][:].bitcast(F32)[:, (s % 2) * 512:(s % 2 + 1) * 512])
            dst = xg[s // 2][:].bitcast(F32)[:, (s % 2) * 512:(s % 2 + 1) * 512]
            copy(eng, dst.rearrange("p (g c u) -> p g c u", g=2, u=2),
                 bank[:].rearrange("p (g u c) -> p g c u", g=2, u=2))

        def quantise_x(part):
            nc.vector.quantize_mx(out=x_codes[part][:].bitcast(FP8X4), scales=x_scales[part][:],
                                  in_=xg[part][:])

        w_codes = {}
        w_scales = {}
        w_grouped = {}

        def transpose_w(wb, engines, q_calls):
            wg = rot.tile([P, 4096], BF16, name="wg", tag="wg", align_bytes=64)
            wg32 = wg[:].bitcast(F32).rearrange(
                "p (g a t c u) -> p g a t c u", g=2, a=2, t=4, c=64, u=2)
            for t in range(4):
                bank = transpose4(w_sb[(wb, t)])
                copy(engines[t], wg32[:, :, :, t, :, :],
                     bank[:].rearrange("p (g u a c) -> p g a c u", g=2, u=2, a=2, c=64))
            w_codes[wb] = rot.tile([P, 1024], U32, name="wc", tag="wc", align_bytes=64)
            w_scales[wb] = rot.tile([P, 1024], U8, name="ws", tag="ws", align_bytes=64)
            w_grouped[wb] = wg
            quantise_w(wb, q_calls)

        def quantise_w(wb, q_calls):
            for c0, n in q_calls:
                nc.vector.quantize_mx(
                    out=w_codes[wb][:, c0:c0 + n].bitcast(FP8X4),
                    scales=w_scales[wb][:, c0:c0 + n],
                    in_=w_grouped[wb][:, 4 * c0:4 * (c0 + n)],
                )

        def mx_pass(acc, s, g, wb, a):
            off = (s % 2) * 256 + g * P
            c0 = g * 512 + a * 256
            nc.tensor.matmul_mx(
                out=acc,
                lhsT=x_codes[s // 2][:, off:off + P].bitcast(FP8X4),
                lhsT_scale=x_scales[s // 2][:, off:off + P],
                rhs=w_codes[wb][:, c0:c0 + 256].bitcast(FP8X4),
                rhs_scale=w_scales[wb][:, c0:c0 + 256],
                start=(g == 0),
                stop=(g == 1),
            )

        o_sb = {}

        def multiply(wb, a, pairs, engines):
            if (wb, a) not in o_sb:
                o_sb[(wb, a)] = keep.tile([P, 2048], F32, name="o_sb%d_%d" % (wb, a))
            o_view = o_sb[(wb, a)][:].rearrange(
                "p (h s q t) -> p s h q t", h=4, s=SETS, q=16, t=4)
            for n, pair in enumerate(pairs):
                acc = new_bank()
                for i in range(2):
                    for g in range(2):
                        mx_pass(acc[:, i * 256:(i + 1) * 256], 2 * pair + i, g, wb, a)
                copy(engines[n], o_view[:, 2 * pair:2 * pair + 2, :, :, :],
                     acc[:].rearrange("p (i t h q) -> p i h q t", i=2, t=4, h=4, q=16))

        def store(wb, a, s0, s1):
            h0 = (wb % 2) * 8 + a * 4
            for b in range(2):
                dst = outs[wb // 2][b, h0:h0 + 4].rearrange("h (q s) d -> q h s d", s=SETS)
                src = o_sb[(wb, a)][b:P:2, :].rearrange("p (h s d) -> p h s d", h=4, s=SETS)
                nc.sync.dma_start(out=dst[:, :, s0:s1, :], in_=src[:, :, s0:s1, :])

        QUARTERS = [(0, 256), (512, 256), (256, 256), (768, 256)]
        HALVES = [(0, 512), (512, 512)]

        def block(wb, engines):
            for a in range(2):
                multiply(wb, a, [0, 1, 2, 3], engines)
                store(wb, a, 0, SETS)

        transpose_x(0, V)
        transpose_x(1, S)
        quantise_x(0)
        transpose_w(0, [V, S, V, S], QUARTERS[0:2])
        transpose_x(2, V)
        transpose_x(3, S)
        quantise_w(0, QUARTERS[2:4])
        quantise_x(1)
        transpose_x(4, S)
        transpose_x(5, S)
        multiply(0, 0, [0], [S])
        multiply(0, 1, [0], [S])
        multiply(0, 0, [1], [S])
        multiply(0, 1, [1], [S])
        quantise_x(2)
        transpose_x(6, V)
        transpose_x(7, V)
        quantise_x(3)
        transpose_w(1, [V, V, S, S], QUARTERS)
        transpose_w(2, [V, V, V, V], HALVES)
        multiply(0, 0, [2, 3], [S, S])
        store(0, 0, 0, SETS)
        multiply(0, 1, [2, 3], [S, S])
        store(0, 1, 0, SETS)
        block(1, [S, S, S, V])
        transpose_w(3, [V, V, V, V], HALVES)
        transpose_w(4, [V, V, V, V], HALVES)
        block(2, [S, S, S, S])
        block(3, [S, S, S, V])
        transpose_w(5, [V, V, V, V], HALVES)
        block(4, [S, S, S, V])
        block(5, [S, V, S, V])
